import numpy as np
import ml_dtypes


def mxq(x, axis, fmt="e4m3"):
    dtype, down = {"e4m3": (ml_dtypes.float8_e4m3fn, 7), "e5m2": (ml_dtypes.float8_e5m2, 14)}[fmt]
    v = np.moveaxis(np.asarray(x, np.float32).astype(ml_dtypes.bfloat16).astype(np.float64), axis, -1)
    blocks = v.reshape(v.shape[:-1] + (-1, 32))
    amax = np.abs(blocks).max(-1, keepdims=True)
    byte = np.maximum(np.where(amax > 0, np.frexp(amax)[1] - 1 + 127, 0) - down, 1)
    scale = np.exp2(byte - 127.0)
    codes = (blocks / scale).astype(np.float32).astype(dtype).astype(np.float64)
    return np.moveaxis((codes * scale).reshape(v.shape), -1, axis)


WIDE = False


def mx_kscale(k):
    if not WIDE:
        return np.ones(k)
    levels = np.array([10, -10, 5, -5, 0])
    if k % 512:
        return np.exp2(np.random.permutation(np.resize(levels, k // 32))).repeat(32)
    a = np.empty((k // 512, 16))
    for p in range(k // 512):
        a[p, :8] = np.random.permutation(np.resize(levels, 8))
        for g in range(8):
            far = levels[np.abs(levels - a[p, g]) >= 10]
            a[p, g + 8] = far[np.random.randint(len(far))]
    return np.exp2(a.ravel()).repeat(32)


BF16 = ml_dtypes.bfloat16


def bf(x):
    return np.asarray(x, np.float32).astype(BF16)


def f64(x):
    return np.asarray(x).astype(np.float64)


B, T, D, H, HD, Q_STRIDE, WINDOW, QKV = 1, 1536, 1024, 16, 64, 4, 128, 3
NW = T // (Q_STRIDE * WINDOW)
SEQ = T // NW


def draw0():
    s = mx_kscale(SEQ)
    t = mx_kscale(D)
    g = np.exp(np.random.standard_normal((B, H, NW, SEQ // Q_STRIDE, SEQ)) * 1.3)
    vd = np.random.standard_normal((B, NW, SEQ, D)) * t / s[:, None]
    return {"attn": bf(g / g.sum(-1, keepdims=True) * s),
            "v": bf(np.ascontiguousarray(vd.reshape(B, NW, SEQ, H, HD).transpose(0, 3, 1, 2, 4))),
            "proj_w": bf(np.random.standard_normal((D, D)) * 5.0 / np.sqrt(D) / t[None, :]),
            "proj_b": bf(np.random.standard_normal(D) * 0.2)}


def core(attn, v, proj_w, proj_b):
    o = mxq(f64(attn), 4, "e4m3") @ mxq(f64(v), 3, "e4m3")
    o = o.transpose(0, 3, 2, 1, 4).reshape(B, -1, H * HD)
    return (mxq(o, 2, "e4m3") @ mxq(f64(proj_w), 1, "e4m3").T) + f64(proj_b)


def e4m3fn_bytes(y):
    return np.clip(np.asarray(y, np.float64), -448.0, 448.0).astype(np.float32).astype(ml_dtypes.float8_e4m3fn).view(np.uint8)


def e4m3fn_values(b):
    return np.asarray(b, np.uint8).view(ml_dtypes.float8_e4m3fn).astype(np.float64)


def setup_inputs():
    d = draw0()
    x0 = np.asarray(d['attn']).astype(np.float64)
    s = (np.max(np.abs(x0), axis=(0, 1, 2, 3), keepdims=True) / 448.0).astype(np.float32)
    out = {}
    for k, v in d.items():
        if k == 'attn':
            out['attn_bytes'] = e4m3fn_bytes(x0 / s.astype(np.float64))
            out['attn_scale'] = s
        else:
            out[k] = v
    return out


def reference(attn_bytes, attn_scale, v, proj_w, proj_b):
    return core(e4m3fn_values(attn_bytes) * attn_scale.astype(np.float64), v, proj_w, proj_b)

@@ -1,0 +1,305 @@
+from contextlib import ExitStack
+
+import concourse.mybir as mybir
+from concourse.masks import make_identity
+
+F32 = mybir.dt.float32
+BF16 = mybir.dt.bfloat16
+U32 = mybir.dt.uint32
+U8 = mybir.dt.uint8
+F8 = mybir.dt.float8_e4m3fn
+X4 = mybir.dt.float8_e4m3fn_x4
+MULT = mybir.AluOpType.mult
+ADD = mybir.AluOpType.add
+
+P = 128
+HEADS, WINDOWS, QUERIES, KEYS, HD = 16, 3, 128, 512, 64
+D = HEADS * HD
+UNITS = WINDOWS * HEADS // 2
+
+FLOPS = 2 * HEADS * WINDOWS * QUERIES * KEYS * HD + 2 * WINDOWS * QUERIES * D * D
+
+
+def tile_hieramaskunitattention_pb_kernel(tc, attn_bytes, attn_scale, v, proj_w, proj_b, out):
+    nc = tc.nc
+    with ExitStack() as ctx:
+        keep = ctx.enter_context(tc.tile_pool(name="keep", bufs=1))
+        bytes_pool = ctx.enter_context(tc.tile_pool(name="bytes_pool", bufs=14))
+        v_pool = ctx.enter_context(tc.tile_pool(name="v_pool", bufs=12))
+        w_pool = ctx.enter_context(tc.tile_pool(name="w_pool", bufs=4))
+        work = ctx.enter_context(tc.tile_pool(name="work", bufs=4))
+        codes_pool = ctx.enter_context(tc.tile_pool(name="codes_pool", bufs=6))
+        turn = ctx.enter_context(tc.psum_pool(name="turn", bufs=4))
+        mix = ctx.enter_context(tc.psum_pool(name="mix", bufs=2))
+        proj = ctx.enter_context(tc.psum_pool(name="proj", bufs=2))
+        ctx.enter_context(tc.manual_schedule())
+
+        ident = keep.tile([P, P], F32)
+        make_identity(nc, ident[:])
+
+        scale_row = attn_scale.rearrange("a b c d k -> (a b c d k)")
+        scale2 = keep.tile([P, 2 * KEYS], F32, align_bytes=64)
+        bias = keep.tile([P, D], BF16)
+        out_rows = out[0].rearrange("(i w) n -> w i n", w=WINDOWS)
+
+        attn_tiles = {}
+        v_tiles = {}
+        w_tiles = {}
+
+        def load_attn(w, h, n):
+            a_bytes = bytes_pool.tile([P, 4, KEYS], U8, align_bytes=64)
+            nc.sync.dma_start(out=a_bytes[:, 0:n, :], in_=attn_bytes[0, h : h + n, w].rearrange("h q k -> q h k"))
+            for i in range(0, n, 2):
+                attn_tiles[8 * w + (h + i) // 2] = a_bytes[:, i : i + 2, :]
+
+        def load_v(w, h):
+            v_raw = v_pool.tile([P, 4, 4, HD], BF16, align_bytes=64)
+            nc.sync.dma_start(
+                out=v_raw[:].rearrange("p h j d -> p h (j d)"),
+                in_=v[0, h : h + 4, w].rearrange("h (p j) d -> p h (j d)", j=4),
+            )
+            for i in (0, 2):
+                v_tiles[8 * w + (h + i) // 2] = v_raw[:, i : i + 2, :, :]
+
+        def load_w(i):
+            w_raw = w_pool.tile([P, 2, D], BF16, align_bytes=64)
+            nc.sync.dma_start(out=w_raw[:], in_=proj_w[256 * i : 256 * (i + 1), :].rearrange("(c n) k -> n c k", c=2))
+            w_tiles[2 * i] = w_raw[:, 0, :]
+            w_tiles[2 * i + 1] = w_raw[:, 1, :]
+
+        load_attn(0, 0, 2)
+        nc.sync.dma_start(out=scale2[:, 0:KEYS], in_=scale_row.partition_broadcast(P))
+        load_v(0, 0)
+        load_attn(0, 2, 2)
+        load_attn(0, 4, 4)
+        load_v(0, 4)
+        load_attn(0, 8, 4)
+        load_w(0)
+        load_v(0, 8)
+        load_attn(0, 12, 4)
+        load_v(0, 12)
+        load_w(1)
+        load_attn(1, 0, 4)
+        load_v(1, 0)
+        load_w(2)
+        load_attn(1, 4, 4)
+        load_v(1, 4)
+        load_w(3)
+        load_attn(1, 8, 4)
+        load_v(1, 8)
+        nc.sync.dma_start(out=bias[:], in_=proj_b.partition_broadcast(P))
+        load_attn(1, 12, 4)
+        load_v(1, 12)
+        for h in range(0, HEADS, 4):
+            load_attn(2, h, 4)
+            load_v(2, h)
+
+        nc.scalar.copy(scale2[:, KEYS : 2 * KEYS], scale2[:, 0:KEYS])
+
+        prods, turned, grouped, a_q, v_grouped, v_q = {}, {}, {}, {}, {}, {}
+        w_turned, w_grouped, w_q = {}, {}, {}
+        mixed, o_turned, o_words, o_grouped, o_q = {}, {}, {}, {}, {}
+
+        def scale_attn(u):
+            prod = work.tile([P, 2 * KEYS], BF16, align_bytes=64)
+            src = attn_tiles[u].rearrange("q h k -> q (h k)").bitcast(F8)
+            width = KEYS if u == 0 else 2 * KEYS
+            for c in range(0, 2 * KEYS, width):
+                nc.vector.tensor_tensor(
+                    out=prod[:, c : c + width], in0=src[:, c : c + width], in1=scale2[:, 0:width], op=MULT
+                )
+            prods[u] = prod
+
+        def turn_attn(u):
+            bank = turn.tile([P, 512], F32)
+            words = prods.pop(u)[:].bitcast(F32)
+            for h in range(2):
+                for j in range(2):
+                    c = 256 * h + 128 * j
+                    nc.tensor.transpose(bank[:, c : c + 128], words[:, 256 * h + j : 256 * (h + 1) : 2], ident[:])
+            turned[u] = bank
+
+        def empty_attn(u):
+            a_grouped = work.tile([P, 1024], BF16, align_bytes=64)
+            nc.scalar.copy(
+                a_grouped[:].bitcast(F32).rearrange("p (h q j) -> p h q j", h=2, j=2),
+                turned.pop(u)[:].rearrange("p (h j q) -> p h q j", h=2, j=2),
+            )
+            grouped[u] = a_grouped
+
+        def quantize_attn(u):
+            a_codes = codes_pool.tile([P, 256], U32, align_bytes=64)
+            a_scales = codes_pool.tile([P, 256], U8, align_bytes=64)
+            nc.vector.quantize_mx(out=a_codes[:].bitcast(X4), scales=a_scales[:], in_=grouped.pop(u)[:])
+            a_q[u] = (a_codes, a_scales)
+
+        def group_v(u):
+            if u % 2 == 0:
+                vg = work.tile([P, 1024], BF16, align_bytes=64)
+                v_grouped[u // 2] = vg
+            i = u % 2
+            nc.scalar.copy(
+                v_grouped[u // 2][:, 512 * i : 512 * (i + 1)].rearrange("p (h d j) -> p h d j", h=2, j=4),
+                v_tiles[u].rearrange("p h j d -> p h d j"),
+            )
+
+        def quantize_v(c):
+            v_codes = codes_pool.tile([P, 256], U32, align_bytes=64)
+            v_scales = codes_pool.tile([P, 256], U8, align_bytes=64)
+            nc.vector.quantize_mx(out=v_codes[:].bitcast(X4), scales=v_scales[:], in_=v_grouped.pop(c)[:])
+            v_q[c] = (v_codes, v_scales)
+
+        def mix_heads(u):
+            a_codes, a_scales = a_q.pop(u)
+            v_codes, v_scales = v_q[u // 2]
+            if u % 4 == 0:
+                o_bank = mix.tile([P, 512], F32)
+                mixed[u // 4] = o_bank
+            for i in range(2):
+                a = slice(128 * i, 128 * (i + 1))
+                b = slice(128 * (u % 2) + 64 * i, 128 * (u % 2) + 64 * (i + 1))
+                o = 128 * (u % 4) + 64 * i
+                nc.tensor.matmul_mx(
+                    out=mixed[u // 4][:, o : o + 64],
+                    lhsT=a_codes[:, a].bitcast(X4),
+                    lhsT_scale=a_scales[:, a],
+                    rhs=v_codes[:, b].bitcast(X4),
+                    rhs_scale=v_scales[:, b],
+                    start=True,
+                    stop=True,
+                )
+
+        def round_o(g):
+            o_bf = work.tile([P, 512], BF16, align_bytes=64)
+            nc.scalar.copy(
+                o_bf[:].rearrange("i (j p e) -> i j p e", j=2, e=2),
+                mixed.pop(g)[:].rearrange("i (p j e) -> i j p e", j=2, e=2),
+            )
+            o_words[g] = o_bf
+
+        def turn_o(g):
+            bank = turn.tile([P, 512], F32)
+            words = o_words.pop(g)[:].bitcast(F32)
+            for j in range(2):
+                nc.tensor.transpose(bank[:, 128 * j : 128 * (j + 1)], words[:, 128 * j : 128 * (j + 1)], ident[:])
+            o_turned[g] = bank
+
+        def empty_o(g):
+            og = work.tile([P, 512], BF16, align_bytes=64)
+            nc.scalar.copy(
+                og[:].bitcast(F32).rearrange("p (i j) -> p i j", j=2),
+                o_turned.pop(g)[:, 0:256].rearrange("p (j i) -> p i j", j=2),
+            )
+            o_grouped[g] = og
+
+        def quantize_o(g):
+            o_codes = codes_pool.tile([P, 128], U32, align_bytes=64)
+            o_scales = codes_pool.tile([P, 128], U8, align_bytes=64)
+            nc.vector.quantize_mx(out=o_codes[:].bitcast(X4), scales=o_scales[:], in_=o_grouped.pop(g)[:])
+            o_q[g] = (o_codes, o_scales)
+
+        def turn_w(i):
+            bank = turn.tile([P, 512], F32)
+            words = w_tiles[i].bitcast(F32)
+            for g in range(2):
+                for j in range(2):
+                    c = 256 * g + 128 * j
+                    nc.tensor.transpose(bank[:, c : c + 128], words[:, 256 * g + j : 256 * (g + 1) : 2], ident[:])
+            w_turned[i] = bank
+
+        def empty_w(i):
+            if i % 4 == 0:
+                wg = keep.tile([P, 2, 2048], BF16, align_bytes=64, name="wg%d" % (i // 4))
+                w_grouped[i // 4] = wg
+            n = i % 4
+            for_g = w_grouped[i // 4][:].rearrange("p g c -> p (g c)").bitcast(F32)
+            nc.scalar.copy(
+                for_g.rearrange("p (g n j) -> p g n j", g=2, j=2)[:, :, 128 * n : 128 * (n + 1), :],
+                w_turned.pop(i)[:].rearrange("p (g j n) -> p g n j", g=2, j=2),
+            )
+
+        def quantize_w(half, g):
+            if g == 0:
+                w_codes = keep.tile([P, 2, 512], U32, align_bytes=64, name="w_codes%d" % half)
+                w_scales = keep.tile([P, 2, 512], U8, align_bytes=64, name="w_scales%d" % half)
+                w_q[half] = (w_codes, w_scales)
+            w_codes, w_scales = w_q[half]
+            nc.vector.quantize_mx(
+                out=w_codes[:, g, :].bitcast(X4), scales=w_scales[:, g, :], in_=w_grouped[half][:, g, :]
+            )
+
+        acc = {}
+
+        def project(w, half, g):
+            if g == 0:
+                y = proj.tile([P, 512], F32)
+                acc[w, half] = y
+            o_codes, o_scales = o_q[2 * w + g]
+            w_codes, w_scales = w_q[half]
+            nc.tensor.matmul_mx(
+                out=acc[w, half][:],
+                lhsT=o_codes[:].bitcast(X4),
+                lhsT_scale=o_scales[:],
+                rhs=w_codes[:, g, :].bitcast(X4),
+                rhs_scale=w_scales[:, g, :],
+                start=(g == 0),
+                stop=(g == 1),
+            )
+
+        def finish(w, half):
+            res = work.tile([P, 512], F32)
+            cols = slice(512 * half, 512 * (half + 1))
+            nc.vector.tensor_tensor(out=res[:], in0=acc.pop((w, half))[:], in1=bias[:, cols], op=ADD)
+            nc.sync.dma_start(out=out_rows[w, :, cols], in_=res[:])
+
+        for s in range(UNITS + 9):
+            if s < UNITS:
+                scale_attn(s)
+            if 1 <= s <= UNITS:
+                empty_attn(s - 1)
+            g = (s - 6) // 4
+            if s >= 6 and (s - 6) % 4 == 0 and g < 6:
+                round_o(g)
+            g = (s - 7) // 4
+            if s >= 7 and (s - 7) % 4 == 0 and g < 6:
+                empty_o(g)
+            if s < UNITS:
+                group_v(s)
+            if 3 <= s <= 17 and s % 2 == 1:
+                empty_w((s - 3) // 2)
+            if s >= 2 and s % 2 == 0 and s // 2 - 1 < UNITS // 2:
+                quantize_v(s // 2 - 1)
+            if 2 <= s < UNITS + 2:
+                quantize_attn(s - 2)
+            g = (s - 8) // 4
+            if s >= 8 and (s - 8) % 4 == 0 and g < 6:
+                quantize_o(g)
+            if s in (10, 11, 18, 19):
+                quantize_w((s - 10) // 8, s % 2)
+            if s < UNITS:
+                turn_attn(s)
+            if 2 <= s <= 16 and s % 2 == 0:
+                turn_w((s - 2) // 2)
+            g = (s - 6) // 4
+            if s >= 6 and (s - 6) % 4 == 0 and g < 6:
+                turn_o(g)
+            if 2 <= s < UNITS + 2:
+                mix_heads(s - 2)
+            if s in (20, 21):
+                project(0, s - 20, 0)
+                project(0, s - 20, 1)
+            if s in (21, 22):
+                finish(0, s - 21)
+            if s in (23, 24):
+                project(1, s - 23, 0)
+                project(1, s - 23, 1)
+            if s in (25, 26):
+                finish(1, s - 25)
+            if s == 27:
+                project(2, 0, 0)
+                project(2, 1, 0)
+            if s == 29:
+                project(2, 0, 1)
+                project(2, 1, 1)
+                finish(2, 0)
+                finish(2, 1)

@@ -25,10 +25,11 @@ def tile_hieramaskunitattention_pb_kernel(tc, attn_bytes, attn_scale, v, proj_w,
     with ExitStack() as ctx:
         keep = ctx.enter_context(tc.tile_pool(name="keep", bufs=1))
         bytes_pool = ctx.enter_context(tc.tile_pool(name="bytes_pool", bufs=14))
-        v_pool = ctx.enter_context(tc.tile_pool(name="v_pool", bufs=12))
+        v_pool = ctx.enter_context(tc.tile_pool(name="v_pool", bufs=13))
         w_pool = ctx.enter_context(tc.tile_pool(name="w_pool", bufs=4))
         work = ctx.enter_context(tc.tile_pool(name="work", bufs=4))
         codes_pool = ctx.enter_context(tc.tile_pool(name="codes_pool", bufs=6))
+        v_stage = ctx.enter_context(tc.tile_pool(name="v_stage", bufs=1))
         turn = ctx.enter_context(tc.psum_pool(name="turn", bufs=4))
         mix = ctx.enter_context(tc.psum_pool(name="mix", bufs=2))
         proj = ctx.enter_context(tc.psum_pool(name="proj", bufs=2))
@@ -36,10 +37,14 @@ def tile_hieramaskunitattention_pb_kernel(tc, attn_bytes, attn_scale, v, proj_w,
 
         ident = keep.tile([P, P], F32)
         make_identity(nc, ident[:])
+        ones = keep.tile([P, P], BF16)
+        nc.vector.memset(ones[:], 1.0)
+        bias_row = keep.tile([P, D], BF16)
+        nc.vector.memset(bias_row[:], 0.0)
 
         scale_row = attn_scale.rearrange("a b c d k -> (a b c d k)")
-        scale2 = keep.tile([P, 2 * KEYS], F32, align_bytes=64)
-        bias = keep.tile([P, D], BF16)
+        scale4 = keep.tile([P, 4], F32, align_bytes=64)
+        bias = keep.tile([P, D], F32)
         out_rows = out[0].rearrange("(i w) n -> w i n", w=WINDOWS)
 
         attn_tiles = {}
@@ -52,13 +57,13 @@ def tile_hieramaskunitattention_pb_kernel(tc, attn_bytes, attn_scale, v, proj_w,
             for i in range(0, n, 2):
                 attn_tiles[8 * w + (h + i) // 2] = a_bytes[:, i : i + 2, :]
 
-        def load_v(w, h):
+        def load_v(w, h, n=4):
             v_raw = v_pool.tile([P, 4, 4, HD], BF16, align_bytes=64)
             nc.sync.dma_start(
-                out=v_raw[:].rearrange("p h j d -> p h (j d)"),
-                in_=v[0, h : h + 4, w].rearrange("h (p j) d -> p h (j d)", j=4),
+                out=v_raw[:, 0:n, :, :].rearrange("p h j d -> p h (j d)"),
+                in_=v[0, h : h + n, w].rearrange("h (p j) d -> p h (j d)", j=4),
             )
-            for i in (0, 2):
+            for i in range(0, n, 2):
                 v_tiles[8 * w + (h + i) // 2] = v_raw[:, i : i + 2, :, :]
 
         def load_w(i):
@@ -67,10 +72,11 @@ def tile_hieramaskunitattention_pb_kernel(tc, attn_bytes, attn_scale, v, proj_w,
             w_tiles[2 * i] = w_raw[:, 0, :]
             w_tiles[2 * i + 1] = w_raw[:, 1, :]
 
+        nc.sync.dma_start(out=scale4[:], in_=scale_row.rearrange("(p t) -> p t", t=4))
         load_attn(0, 0, 2)
-        nc.sync.dma_start(out=scale2[:, 0:KEYS], in_=scale_row.partition_broadcast(P))
-        load_v(0, 0)
+        load_v(0, 0, 2)
         load_attn(0, 2, 2)
+        load_v(0, 2, 2)
         load_attn(0, 4, 4)
         load_v(0, 4)
         load_attn(0, 8, 4)
@@ -87,77 +93,86 @@ def tile_hieramaskunitattention_pb_kernel(tc, attn_bytes, attn_scale, v, proj_w,
         load_w(3)
         load_attn(1, 8, 4)
         load_v(1, 8)
-        nc.sync.dma_start(out=bias[:], in_=proj_b.partition_broadcast(P))
+        nc.sync.dma_start(out=bias_row[0:1, :], in_=proj_b.rearrange("(o n) -> o n", o=1))
         load_attn(1, 12, 4)
         load_v(1, 12)
         for h in range(0, HEADS, 4):
             load_attn(2, h, 4)
             load_v(2, h)
 
-        nc.scalar.copy(scale2[:, KEYS : 2 * KEYS], scale2[:, 0:KEYS])
+        def spread_bias(half):
+            bias_bank = proj.tile([P, 512], F32, name="y")
+            cols = slice(512 * half, 512 * (half + 1))
+            nc.tensor.matmul(bias_bank[:], lhsT=ones[:], rhs=bias_row[:, cols], start=True, stop=True)
+            nc.scalar.copy(bias[:, cols], bias_bank[:])
 
         prods, turned, grouped, a_q, v_grouped, v_q = {}, {}, {}, {}, {}, {}
         w_turned, w_grouped, w_q = {}, {}, {}
         mixed, o_turned, o_words, o_grouped, o_q = {}, {}, {}, {}, {}
 
-        def scale_attn(u):
-            prod = work.tile([P, 2 * KEYS], BF16, align_bytes=64)
+        def widen_attn(u):
+            wide = work.tile([P, 2 * KEYS], BF16, align_bytes=64)
             src = attn_tiles[u].rearrange("q h k -> q (h k)").bitcast(F8)
             width = KEYS if u == 0 else 2 * KEYS
             for c in range(0, 2 * KEYS, width):
-                nc.vector.tensor_tensor(
-                    out=prod[:, c : c + width], in0=src[:, c : c + width], in1=scale2[:, 0:width], op=MULT
-                )
-            prods[u] = prod
+                nc.scalar.copy(wide[:, c : c + width], src[:, c : c + width])
+            prods[u] = wide
 
         def turn_attn(u):
             bank = turn.tile([P, 512], F32)
             words = prods.pop(u)[:].bitcast(F32)
             for h in range(2):
                 for j in range(2):
-                    c = 256 * h + 128 * j
+                    c = 256 * j + 128 * h
                     nc.tensor.transpose(bank[:, c : c + 128], words[:, 256 * h + j : 256 * (h + 1) : 2], ident[:])
             turned[u] = bank
 
-        def empty_attn(u):
+        def scale_attn(u, h0=0, n=2):
             a_grouped = work.tile([P, 1024], BF16, align_bytes=64)
-            nc.scalar.copy(
-                a_grouped[:].bitcast(F32).rearrange("p (h q j) -> p h q j", h=2, j=2),
-                turned.pop(u)[:].rearrange("p (h j q) -> p h q j", h=2, j=2),
+            lo, hi = 128 * h0, 128 * (h0 + n)
+            nc.vector.tensor_tensor(
+                out=a_grouped[:, 0 : 512 * n].rearrange("p (q j e) -> p q j e", j=2, e=2),
+                in0=turned[u][:].bitcast(BF16).rearrange("p (j q e) -> p q j e", j=2, e=2)[:, lo:hi, :, :],
+                in1=scale4[:].unsqueeze(1).to_broadcast([P, hi - lo, 4]).rearrange("p q (j e) -> p q j e", e=2),
+                op=MULT,
             )
-            grouped[u] = a_grouped
+            grouped[u, h0] = a_grouped
 
-        def quantize_attn(u):
+        def quantize_attn(u, h0=0, n=2):
             a_codes = codes_pool.tile([P, 256], U32, align_bytes=64)
             a_scales = codes_pool.tile([P, 256], U8, align_bytes=64)
-            nc.vector.quantize_mx(out=a_codes[:].bitcast(X4), scales=a_scales[:], in_=grouped.pop(u)[:])
-            a_q[u] = (a_codes, a_scales)
+            nc.vector.quantize_mx(
+                out=a_codes[:, 0 : 128 * n].bitcast(X4),
+                scales=a_scales[:, 0 : 128 * n],
+                in_=grouped.pop((u, h0))[:, 0 : 512 * n],
+            )
+            a_q[u, h0] = (a_codes, a_scales)
 
         def group_v(u):
-            if u % 2 == 0:
-                vg = work.tile([P, 1024], BF16, align_bytes=64)
-                v_grouped[u // 2] = vg
-            i = u % 2
-            nc.scalar.copy(
-                v_grouped[u // 2][:, 512 * i : 512 * (i + 1)].rearrange("p (h d j) -> p h d j", h=2, j=4),
-                v_tiles[u].rearrange("p h j d -> p h d j"),
-            )
+            vg = v_stage.tile([P, 512], BF16, align_bytes=64)
+            dst = vg[:].rearrange("p (h d j) -> p h d j", h=2, j=4)
+            src = v_tiles[u].rearrange("p h j d -> p h d j")
+            if u == 0:
+                nc.vector.tensor_copy(dst, src)
+            else:
+                nc.gpsimd.tensor_scalar(dst, src, 1.0, 0.0, MULT, ADD)
+            v_grouped[u] = vg
 
-        def quantize_v(c):
-            v_codes = codes_pool.tile([P, 256], U32, align_bytes=64)
-            v_scales = codes_pool.tile([P, 256], U8, align_bytes=64)
-            nc.vector.quantize_mx(out=v_codes[:].bitcast(X4), scales=v_scales[:], in_=v_grouped.pop(c)[:])
-            v_q[c] = (v_codes, v_scales)
+        def quantize_v(u):
+            v_codes = codes_pool.tile([P, 128], U32, align_bytes=64)
+            v_scales = codes_pool.tile([P, 128], U8, align_bytes=64)
+            nc.vector.quantize_mx(out=v_codes[:].bitcast(X4), scales=v_scales[:], in_=v_grouped.pop(u)[:])
+            v_q[u] = (v_codes, v_scales)
 
-        def mix_heads(u):
-            a_codes, a_scales = a_q.pop(u)
-            v_codes, v_scales = v_q[u // 2]
-            if u % 4 == 0:
+        def mix_heads(u, h0=0, n=2):
+            a_codes, a_scales = a_q.pop((u, h0))
+            v_codes, v_scales = v_q[u]
+            if u % 4 == 0 and h0 == 0:
                 o_bank = mix.tile([P, 512], F32)
                 mixed[u // 4] = o_bank
-            for i in range(2):
-                a = slice(128 * i, 128 * (i + 1))
-                b = slice(128 * (u % 2) + 64 * i, 128 * (u % 2) + 64 * (i + 1))
+            for i in range(h0, h0 + n):
+                a = slice(128 * (i - h0), 128 * (i - h0 + 1))
+                b = slice(64 * i, 64 * (i + 1))
                 o = 128 * (u % 4) + 64 * i
                 nc.tensor.matmul_mx(
                     out=mixed[u // 4][:, o : o + 64],
@@ -169,13 +184,16 @@ def tile_hieramaskunitattention_pb_kernel(tc, attn_bytes, attn_scale, v, proj_w,
                     stop=True,
                 )
 
-        def round_o(g):
-            o_bf = work.tile([P, 512], BF16, align_bytes=64)
+        def round_o(u, n):
+            g = u // 4
+            if u % 4 == 0:
+                o_bf = work.tile([P, 512], BF16, align_bytes=64)
+                o_words[g] = o_bf
+            lo, hi = 32 * (u % 4), 32 * (u % 4 + n)
             nc.scalar.copy(
-                o_bf[:].rearrange("i (j p e) -> i j p e", j=2, e=2),
-                mixed.pop(g)[:].rearrange("i (p j e) -> i j p e", j=2, e=2),
+                o_words[g][:].rearrange("i (j p e) -> i j p e", j=2, e=2)[:, :, lo:hi, :],
+                mixed[g][:].rearrange("i (p j e) -> i j p e", j=2, e=2)[:, :, lo:hi, :],
             )
-            o_words[g] = o_bf
 
         def turn_o(g):
             bank = turn.tile([P, 512], F32)
@@ -252,54 +270,70 @@ def tile_hieramaskunitattention_pb_kernel(tc, attn_bytes, attn_scale, v, proj_w,
             nc.vector.tensor_tensor(out=res[:], in0=acc.pop((w, half))[:], in1=bias[:, cols], op=ADD)
             nc.sync.dma_start(out=out_rows[w, :, cols], in_=res[:])
 
-        for s in range(UNITS + 9):
-            if s < UNITS:
+        last = UNITS - 1
+        widen_attn(0)
+        widen_attn(1)
+        group_v(0)
+        turn_attn(0)
+        for s in range(UNITS):
+            if s + 2 < UNITS:
+                widen_attn(s + 2)
+            quantize_v(s)
+            if s < last:
+                group_v(s + 1)
                 scale_attn(s)
-            if 1 <= s <= UNITS:
-                empty_attn(s - 1)
-            g = (s - 6) // 4
-            if s >= 6 and (s - 6) % 4 == 0 and g < 6:
-                round_o(g)
-            g = (s - 7) // 4
-            if s >= 7 and (s - 7) % 4 == 0 and g < 6:
+            else:
+                scale_attn(s, 0, 1)
+                scale_attn(s, 1, 1)
+            if s >= 3 and s % 2 == 1:
+                round_o(s - 3, 2)
+            g, r = divmod(s - 7, 4)
+            if s >= 7 and r == 0:
                 empty_o(g)
-            if s < UNITS:
-                group_v(s)
             if 3 <= s <= 17 and s % 2 == 1:
                 empty_w((s - 3) // 2)
-            if s >= 2 and s % 2 == 0 and s // 2 - 1 < UNITS // 2:
-                quantize_v(s // 2 - 1)
-            if 2 <= s < UNITS + 2:
-                quantize_attn(s - 2)
-            g = (s - 8) // 4
-            if s >= 8 and (s - 8) % 4 == 0 and g < 6:
+            if s >= 1:
+                quantize_attn(s - 1)
+            g, r = divmod(s - 8, 4)
+            if s >= 8 and r == 0:
                 quantize_o(g)
             if s in (10, 11, 18, 19):
                 quantize_w((s - 10) // 8, s % 2)
-            if s < UNITS:
-                turn_attn(s)
+            if s < last:
+                turn_attn(s + 1)
             if 2 <= s <= 16 and s % 2 == 0:
                 turn_w((s - 2) // 2)
-            g = (s - 6) // 4
-            if s >= 6 and (s - 6) % 4 == 0 and g < 6:
+            g, r = divmod(s - 6, 4)
+            if s >= 6 and r == 0:
                 turn_o(g)
-            if 2 <= s < UNITS + 2:
+            if s >= 2 and s % 2 == 0:
                 mix_heads(s - 2)
-            if s in (20, 21):
-                project(0, s - 20, 0)
-                project(0, s - 20, 1)
-            if s in (21, 22):
-                finish(0, s - 21)
-            if s in (23, 24):
-                project(1, s - 23, 0)
-                project(1, s - 23, 1)
-            if s in (25, 26):
-                finish(1, s - 25)
-            if s == 27:
-                project(2, 0, 0)
-                project(2, 1, 0)
-            if s == 29:
-                project(2, 0, 1)
-                project(2, 1, 1)
-                finish(2, 0)
-                finish(2, 1)
+                mix_heads(s - 1)
+            if s in (11, 12):
+                spread_bias(s - 11)
+            if s in (14, 20):
+                project(0, (s - 14) // 6, 0)
+                project(0, (s - 14) // 6, 1)
+            if s in (16, 21):
+                finish(0, (s - 16) // 5)
+            if s >= 22:
+                project(1, s - 22, 0)
+                project(1, s - 22, 1)
+        mix_heads(last - 1)
+        quantize_attn(last, 0, 1)
+        quantize_attn(last, 1, 1)
+        quantize_o(4)
+        mix_heads(last, 0, 1)
+        mix_heads(last, 1, 1)
+        round_o(last - 1, 2)
+        finish(1, 0)
+        turn_o(5)
+        project(2, 0, 0)
+        empty_o(5)
+        finish(1, 1)
+        project(2, 1, 0)
+        quantize_o(5)
+        project(2, 0, 1)
+        project(2, 1, 1)
+        finish(2, 0)
+        finish(2, 1)

@@ -15,6 +15,8 @@ ADD = mybir.AluOpType.add
 P = 128
 HEADS, WINDOWS, QUERIES, KEYS, HD = 16, 3, 128, 512, 64
 D = HEADS * HD
+LEAD = 3
+TL = 2
 UNITS = WINDOWS * HEADS // 2
 
 FLOPS = 2 * HEADS * WINDOWS * QUERIES * KEYS * HD + 2 * WINDOWS * QUERIES * D * D
@@ -27,9 +29,8 @@ def tile_hieramaskunitattention_pb_kernel(tc, attn_bytes, attn_scale, v, proj_w,
         bytes_pool = ctx.enter_context(tc.tile_pool(name="bytes_pool", bufs=14))
         v_pool = ctx.enter_context(tc.tile_pool(name="v_pool", bufs=13))
         w_pool = ctx.enter_context(tc.tile_pool(name="w_pool", bufs=4))
-        work = ctx.enter_context(tc.tile_pool(name="work", bufs=4))
+        work = ctx.enter_context(tc.tile_pool(name="work", bufs=6))
         codes_pool = ctx.enter_context(tc.tile_pool(name="codes_pool", bufs=6))
-        v_stage = ctx.enter_context(tc.tile_pool(name="v_stage", bufs=1))
         turn = ctx.enter_context(tc.psum_pool(name="turn", bufs=4))
         mix = ctx.enter_context(tc.psum_pool(name="mix", bufs=2))
         proj = ctx.enter_context(tc.psum_pool(name="proj", bufs=2))
@@ -115,7 +116,8 @@ def tile_hieramaskunitattention_pb_kernel(tc, attn_bytes, attn_scale, v, proj_w,
             src = attn_tiles[u].rearrange("q h k -> q (h k)").bitcast(F8)
             width = KEYS if u == 0 else 2 * KEYS
             for c in range(0, 2 * KEYS, width):
-                nc.scalar.copy(wide[:, c : c + width], src[:, c : c + width])
+                copy = nc.vector.tensor_copy if u == 0 and c == 0 else nc.scalar.copy
+                copy(wide[:, c : c + width], src[:, c : c + width])
             prods[u] = wide
 
         def turn_attn(u):
@@ -128,50 +130,56 @@ def tile_hieramaskunitattention_pb_kernel(tc, attn_bytes, attn_scale, v, proj_w,
             turned[u] = bank
 
         def scale_attn(u, h0=0, n=2):
-            a_grouped = work.tile([P, 1024], BF16, align_bytes=64)
+            if u % 2 == 0:
+                a_grouped = work.tile([P, 2048], BF16, align_bytes=64)
+                grouped[u // 2] = a_grouped
             lo, hi = 128 * h0, 128 * (h0 + n)
+            first = 1024 * (u % 2) + 512 * h0
             nc.vector.tensor_tensor(
-                out=a_grouped[:, 0 : 512 * n].rearrange("p (q j e) -> p q j e", j=2, e=2),
+                out=grouped[u // 2][:, first : first + 512 * n].rearrange("p (q j e) -> p q j e", j=2, e=2),
                 in0=turned[u][:].bitcast(BF16).rearrange("p (j q e) -> p q j e", j=2, e=2)[:, lo:hi, :, :],
                 in1=scale4[:].unsqueeze(1).to_broadcast([P, hi - lo, 4]).rearrange("p q (j e) -> p q j e", e=2),
                 op=MULT,
             )
-            grouped[u, h0] = a_grouped
 
-        def quantize_attn(u, h0=0, n=2):
-            a_codes = codes_pool.tile([P, 256], U32, align_bytes=64)
-            a_scales = codes_pool.tile([P, 256], U8, align_bytes=64)
+        def quantize_attn(c, h0=0, n=4):
+            if h0 == 0:
+                a_codes = codes_pool.tile([P, 512], U32, align_bytes=64)
+                a_scales = codes_pool.tile([P, 512], U8, align_bytes=64)
+                a_q[c] = (a_codes, a_scales)
+            a_codes, a_scales = a_q[c]
+            cols = slice(128 * h0, 128 * (h0 + n))
             nc.vector.quantize_mx(
-                out=a_codes[:, 0 : 128 * n].bitcast(X4),
-                scales=a_scales[:, 0 : 128 * n],
-                in_=grouped.pop((u, h0))[:, 0 : 512 * n],
+                out=a_codes[:, cols].bitcast(X4),
+                scales=a_scales[:, cols],
+                in_=grouped[c][:, 512 * h0 : 512 * (h0 + n)],
             )
-            a_q[u, h0] = (a_codes, a_scales)
+
+        v_stage = keep.tile([P, 512], BF16, align_bytes=64)
 
         def group_v(u):
-            vg = v_stage.tile([P, 512], BF16, align_bytes=64)
-            dst = vg[:].rearrange("p (h d j) -> p h d j", h=2, j=4)
+            dst = v_stage[:].rearrange("p (h d j) -> p h d j", h=2, j=4)
             src = v_tiles[u].rearrange("p h j d -> p h d j")
             if u == 0:
                 nc.vector.tensor_copy(dst, src)
             else:
                 nc.gpsimd.tensor_scalar(dst, src, 1.0, 0.0, MULT, ADD)
-            v_grouped[u] = vg
 
         def quantize_v(u):
             v_codes = codes_pool.tile([P, 128], U32, align_bytes=64)
             v_scales = codes_pool.tile([P, 128], U8, align_bytes=64)
-            nc.vector.quantize_mx(out=v_codes[:].bitcast(X4), scales=v_scales[:], in_=v_grouped.pop(u)[:])
+            nc.vector.quantize_mx(out=v_codes[:].bitcast(X4), scales=v_scales[:], in_=v_stage[:])
             v_q[u] = (v_codes, v_scales)
 
         def mix_heads(u, h0=0, n=2):
-            a_codes, a_scales = a_q.pop((u, h0))
+            a_codes, a_scales = a_q[u // 2]
             v_codes, v_scales = v_q[u]
             if u % 4 == 0 and h0 == 0:
                 o_bank = mix.tile([P, 512], F32)
                 mixed[u // 4] = o_bank
             for i in range(h0, h0 + n):
-                a = slice(128 * (i - h0), 128 * (i - h0 + 1))
+                head = 2 * (u % 2) + i
+                a = slice(128 * head, 128 * (head + 1))
                 b = slice(64 * i, 64 * (i + 1))
                 o = 128 * (u % 4) + 64 * i
                 nc.tensor.matmul_mx(
@@ -273,11 +281,16 @@ def tile_hieramaskunitattention_pb_kernel(tc, attn_bytes, attn_scale, v, proj_w,
         last = UNITS - 1
         widen_attn(0)
         widen_attn(1)
+        for u in range(2, LEAD):
+            widen_attn(u)
         group_v(0)
-        turn_attn(0)
+        for u in range(TL):
+            turn_attn(u)
         for s in range(UNITS):
-            if s + 2 < UNITS:
-                widen_attn(s + 2)
+            if s + LEAD < UNITS:
+                widen_attn(s + LEAD)
+            if 3 <= s <= 17 and s % 2 == 1:
+                empty_w((s - 3) // 2)
             quantize_v(s)
             if s < last:
                 group_v(s + 1)
@@ -290,17 +303,17 @@ def tile_hieramaskunitattention_pb_kernel(tc, attn_bytes, attn_scale, v, proj_w,
             g, r = divmod(s - 7, 4)
             if s >= 7 and r == 0:
                 empty_o(g)
-            if 3 <= s <= 17 and s % 2 == 1:
-                empty_w((s - 3) // 2)
-            if s >= 1:
-                quantize_attn(s - 1)
-            g, r = divmod(s - 8, 4)
-            if s >= 8 and r == 0:
+            if s >= 2 and s % 2 == 0:
+                quantize_attn(s // 2 - 1)
+            if s == last:
+                quantize_attn(s // 2, 0, 2)
+            g, r = divmod(s - 9, 4)
+            if s >= 9 and r == 0:
                 quantize_o(g)
-            if s in (10, 11, 18, 19):
-                quantize_w((s - 10) // 8, s % 2)
-            if s < last:
-                turn_attn(s + 1)
+            if s in (11, 12, 19, 20):
+                quantize_w((s - 11) // 8, (s - 11) % 2)
+            if s + TL < UNITS:
+                turn_attn(s + TL)
             if 2 <= s <= 16 and s % 2 == 0:
                 turn_w((s - 2) // 2)
             g, r = divmod(s - 6, 4)
@@ -311,17 +324,20 @@ def tile_hieramaskunitattention_pb_kernel(tc, attn_bytes, attn_scale, v, proj_w,
                 mix_heads(s - 1)
             if s in (11, 12):
                 spread_bias(s - 11)
-            if s in (14, 20):
-                project(0, (s - 14) // 6, 0)
-                project(0, (s - 14) // 6, 1)
-            if s in (16, 21):
-                finish(0, (s - 16) // 5)
-            if s >= 22:
-                project(1, s - 22, 0)
-                project(1, s - 22, 1)
+            if s in (14, 21):
+                project(0, (s - 14) // 7, 0)
+                project(0, (s - 14) // 7, 1)
+            if s in (16, 22):
+                finish(0, (s - 16) // 6)
+            if s == 22:
+                project(1, 0, 0)
+                project(1, 0, 1)
+            if s == 23:
+                project(1, 1, 0)
+                project(1, 1, 1)
         mix_heads(last - 1)
-        quantize_attn(last, 0, 1)
-        quantize_attn(last, 1, 1)
+        quantize_attn(last // 2, 2, 1)
+        quantize_attn(last // 2, 3, 1)
         quantize_o(4)
         mix_heads(last, 0, 1)
         mix_heads(last, 1, 1)

from contextlib import ExitStack

import concourse.mybir as mybir
from concourse.masks import make_identity

F32 = mybir.dt.float32
BF16 = mybir.dt.bfloat16
U32 = mybir.dt.uint32
U8 = mybir.dt.uint8
F8 = mybir.dt.float8_e4m3fn
X4 = mybir.dt.float8_e4m3fn_x4
MULT = mybir.AluOpType.mult
ADD = mybir.AluOpType.add

P = 128
HEADS, WINDOWS, QUERIES, KEYS, HD = 16, 3, 128, 512, 64
D = HEADS * HD
LEAD = 3
TL = 2
UNITS = WINDOWS * HEADS // 2

FLOPS = 2 * HEADS * WINDOWS * QUERIES * KEYS * HD + 2 * WINDOWS * QUERIES * D * D


def tile_hieramaskunitattention_pb_kernel(tc, attn_bytes, attn_scale, v, proj_w, proj_b, out):
    nc = tc.nc
    with ExitStack() as ctx:
        keep = ctx.enter_context(tc.tile_pool(name="keep", bufs=1))
        bytes_pool = ctx.enter_context(tc.tile_pool(name="bytes_pool", bufs=14))
        v_pool = ctx.enter_context(tc.tile_pool(name="v_pool", bufs=13))
        w_pool = ctx.enter_context(tc.tile_pool(name="w_pool", bufs=4))
        work = ctx.enter_context(tc.tile_pool(name="work", bufs=6))
        codes_pool = ctx.enter_context(tc.tile_pool(name="codes_pool", bufs=6))
        turn = ctx.enter_context(tc.psum_pool(name="turn", bufs=4))
        mix = ctx.enter_context(tc.psum_pool(name="mix", bufs=2))
        proj = ctx.enter_context(tc.psum_pool(name="proj", bufs=2))
        ctx.enter_context(tc.manual_schedule())

        ident = keep.tile([P, P], F32)
        make_identity(nc, ident[:])
        ones = keep.tile([P, P], BF16)
        nc.vector.memset(ones[:], 1.0)
        bias_row = keep.tile([P, D], BF16)
        nc.vector.memset(bias_row[:], 0.0)

        scale_row = attn_scale.rearrange("a b c d k -> (a b c d k)")
        scale4 = keep.tile([P, 4], F32, align_bytes=64)
        bias = keep.tile([P, D], F32)
        out_rows = out[0].rearrange("(i w) n -> w i n", w=WINDOWS)

        attn_tiles = {}
        v_tiles = {}
        w_tiles = {}

        def load_attn(w, h, n):
            a_bytes = bytes_pool.tile([P, 4, KEYS], U8, align_bytes=64)
            nc.sync.dma_start(out=a_bytes[:, 0:n, :], in_=attn_bytes[0, h : h + n, w].rearrange("h q k -> q h k"))
            for i in range(0, n, 2):
                attn_tiles[8 * w + (h + i) // 2] = a_bytes[:, i : i + 2, :]

        def load_v(w, h, n=4):
            v_raw = v_pool.tile([P, 4, 4, HD], BF16, align_bytes=64)
            nc.sync.dma_start(
                out=v_raw[:, 0:n, :, :].rearrange("p h j d -> p h (j d)"),
                in_=v[0, h : h + n, w].rearrange("h (p j) d -> p h (j d)", j=4),
            )
            for i in range(0, n, 2):
                v_tiles[8 * w + (h + i) // 2] = v_raw[:, i : i + 2, :, :]

        def load_w(i):
            w_raw = w_pool.tile([P, 2, D], BF16, align_bytes=64)
            nc.sync.dma_start(out=w_raw[:], in_=proj_w[256 * i : 256 * (i + 1), :].rearrange("(c n) k -> n c k", c=2))
            w_tiles[2 * i] = w_raw[:, 0, :]
            w_tiles[2 * i + 1] = w_raw[:, 1, :]

        nc.sync.dma_start(out=scale4[:], in_=scale_row.rearrange("(p t) -> p t", t=4))
        load_attn(0, 0, 2)
        load_v(0, 0, 2)
        load_attn(0, 2, 2)
        load_v(0, 2, 2)
        load_attn(0, 4, 4)
        load_v(0, 4)
        load_attn(0, 8, 4)
        load_w(0)
        load_v(0, 8)
        load_attn(0, 12, 4)
        load_v(0, 12)
        load_w(1)
        load_attn(1, 0, 4)
        load_v(1, 0)
        load_w(2)
        load_attn(1, 4, 4)
        load_v(1, 4)
        load_w(3)
        load_attn(1, 8, 4)
        load_v(1, 8)
        nc.sync.dma_start(out=bias_row[0:1, :], in_=proj_b.rearrange("(o n) -> o n", o=1))
        load_attn(1, 12, 4)
        load_v(1, 12)
        for h in range(0, HEADS, 4):
            load_attn(2, h, 4)
            load_v(2, h)

        def spread_bias(half):
            bias_bank = proj.tile([P, 512], F32, name="y")
            cols = slice(512 * half, 512 * (half + 1))
            nc.tensor.matmul(bias_bank[:], lhsT=ones[:], rhs=bias_row[:, cols], start=True, stop=True)
            nc.scalar.copy(bias[:, cols], bias_bank[:])

        prods, turned, grouped, a_q, v_grouped, v_q = {}, {}, {}, {}, {}, {}
        w_turned, w_grouped, w_q = {}, {}, {}
        mixed, o_turned, o_words, o_grouped, o_q = {}, {}, {}, {}, {}

        def widen_attn(u):
            wide = work.tile([P, 2 * KEYS], BF16, align_bytes=64)
            src = attn_tiles[u].rearrange("q h k -> q (h k)").bitcast(F8)
            width = KEYS if u == 0 else 2 * KEYS
            for c in range(0, 2 * KEYS, width):
                copy = nc.vector.tensor_copy if u == 0 and c == 0 else nc.scalar.copy
                copy(wide[:, c : c + width], src[:, c : c + width])
            prods[u] = wide

        def turn_attn(u):
            bank = turn.tile([P, 512], F32)
            words = prods.pop(u)[:].bitcast(F32)
            for h in range(2):
                for j in range(2):
                    c = 256 * j + 128 * h
                    nc.tensor.transpose(bank[:, c : c + 128], words[:, 256 * h + j : 256 * (h + 1) : 2], ident[:])
            turned[u] = bank

        def scale_attn(u, h0=0, n=2):
            if u % 2 == 0:
                a_grouped = work.tile([P, 2048], BF16, align_bytes=64)
                grouped[u // 2] = a_grouped
            lo, hi = 128 * h0, 128 * (h0 + n)
            first = 1024 * (u % 2) + 512 * h0
            nc.vector.tensor_tensor(
                out=grouped[u // 2][:, first : first + 512 * n].rearrange("p (q j e) -> p q j e", j=2, e=2),
                in0=turned[u][:].bitcast(BF16).rearrange("p (j q e) -> p q j e", j=2, e=2)[:, lo:hi, :, :],
                in1=scale4[:].unsqueeze(1).to_broadcast([P, hi - lo, 4]).rearrange("p q (j e) -> p q j e", e=2),
                op=MULT,
            )

        def quantize_attn(c, h0=0, n=4):
            if h0 == 0:
                a_codes = codes_pool.tile([P, 512], U32, align_bytes=64)
                a_scales = codes_pool.tile([P, 512], U8, align_bytes=64)
                a_q[c] = (a_codes, a_scales)
            a_codes, a_scales = a_q[c]
            cols = slice(128 * h0, 128 * (h0 + n))
            nc.vector.quantize_mx(
                out=a_codes[:, cols].bitcast(X4),
                scales=a_scales[:, cols],
                in_=grouped[c][:, 512 * h0 : 512 * (h0 + n)],
            )

        v_stage = keep.tile([P, 512], BF16, align_bytes=64)

        def group_v(u):
            dst = v_stage[:].rearrange("p (h d j) -> p h d j", h=2, j=4)
            src = v_tiles[u].rearrange("p h j d -> p h d j")
            if u == 0:
                nc.vector.tensor_copy(dst, src)
            else:
                nc.gpsimd.tensor_scalar(dst, src, 1.0, 0.0, MULT, ADD)

        def quantize_v(u):
            v_codes = codes_pool.tile([P, 128], U32, align_bytes=64)
            v_scales = codes_pool.tile([P, 128], U8, align_bytes=64)
            nc.vector.quantize_mx(out=v_codes[:].bitcast(X4), scales=v_scales[:], in_=v_stage[:])
            v_q[u] = (v_codes, v_scales)

        def mix_heads(u, h0=0, n=2):
            a_codes, a_scales = a_q[u // 2]
            v_codes, v_scales = v_q[u]
            if u % 4 == 0 and h0 == 0:
                o_bank = mix.tile([P, 512], F32)
                mixed[u // 4] = o_bank
            for i in range(h0, h0 + n):
                head = 2 * (u % 2) + i
                a = slice(128 * head, 128 * (head + 1))
                b = slice(64 * i, 64 * (i + 1))
                o = 128 * (u % 4) + 64 * i
                nc.tensor.matmul_mx(
                    out=mixed[u // 4][:, o : o + 64],
                    lhsT=a_codes[:, a].bitcast(X4),
                    lhsT_scale=a_scales[:, a],
                    rhs=v_codes[:, b].bitcast(X4),
                    rhs_scale=v_scales[:, b],
                    start=True,
                    stop=True,
                )

        def round_o(u, n):
            g = u // 4
            if u % 4 == 0:
                o_bf = work.tile([P, 512], BF16, align_bytes=64)
                o_words[g] = o_bf
            lo, hi = 32 * (u % 4), 32 * (u % 4 + n)
            nc.scalar.copy(
                o_words[g][:].rearrange("i (j p e) -> i j p e", j=2, e=2)[:, :, lo:hi, :],
                mixed[g][:].rearrange("i (p j e) -> i j p e", j=2, e=2)[:, :, lo:hi, :],
            )

        def turn_o(g):
            bank = turn.tile([P, 512], F32)
            words = o_words.pop(g)[:].bitcast(F32)
            for j in range(2):
                nc.tensor.transpose(bank[:, 128 * j : 128 * (j + 1)], words[:, 128 * j : 128 * (j + 1)], ident[:])
            o_turned[g] = bank

        def empty_o(g):
            og = work.tile([P, 512], BF16, align_bytes=64)
            nc.scalar.copy(
                og[:].bitcast(F32).rearrange("p (i j) -> p i j", j=2),
                o_turned.pop(g)[:, 0:256].rearrange("p (j i) -> p i j", j=2),
            )
            o_grouped[g] = og

        def quantize_o(g):
            o_codes = codes_pool.tile([P, 128], U32, align_bytes=64)
            o_scales = codes_pool.tile([P, 128], U8, align_bytes=64)
            nc.vector.quantize_mx(out=o_codes[:].bitcast(X4), scales=o_scales[:], in_=o_grouped.pop(g)[:])
            o_q[g] = (o_codes, o_scales)

        def turn_w(i):
            bank = turn.tile([P, 512], F32)
            words = w_tiles[i].bitcast(F32)
            for g in range(2):
                for j in range(2):
                    c = 256 * g + 128 * j
                    nc.tensor.transpose(bank[:, c : c + 128], words[:, 256 * g + j : 256 * (g + 1) : 2], ident[:])
            w_turned[i] = bank

        def empty_w(i):
            if i % 4 == 0:
                wg = keep.tile([P, 2, 2048], BF16, align_bytes=64, name="wg%d" % (i // 4))
                w_grouped[i // 4] = wg
            n = i % 4
            for_g = w_grouped[i // 4][:].rearrange("p g c -> p (g c)").bitcast(F32)
            nc.scalar.copy(
                for_g.rearrange("p (g n j) -> p g n j", g=2, j=2)[:, :, 128 * n : 128 * (n + 1), :],
                w_turned.pop(i)[:].rearrange("p (g j n) -> p g n j", g=2, j=2),
            )

        def quantize_w(half, g):
            if g == 0:
                w_codes = keep.tile([P, 2, 512], U32, align_bytes=64, name="w_codes%d" % half)
                w_scales = keep.tile([P, 2, 512], U8, align_bytes=64, name="w_scales%d" % half)
                w_q[half] = (w_codes, w_scales)
            w_codes, w_scales = w_q[half]
            nc.vector.quantize_mx(
                out=w_codes[:, g, :].bitcast(X4), scales=w_scales[:, g, :], in_=w_grouped[half][:, g, :]
            )

        acc = {}

        def project(w, half, g):
            if g == 0:
                y = proj.tile([P, 512], F32)
                acc[w, half] = y
            o_codes, o_scales = o_q[2 * w + g]
            w_codes, w_scales = w_q[half]
            nc.tensor.matmul_mx(
                out=acc[w, half][:],
                lhsT=o_codes[:].bitcast(X4),
                lhsT_scale=o_scales[:],
                rhs=w_codes[:, g, :].bitcast(X4),
                rhs_scale=w_scales[:, g, :],
                start=(g == 0),
                stop=(g == 1),
            )

        def finish(w, half):
            res = work.tile([P, 512], F32)
            cols = slice(512 * half, 512 * (half + 1))
            nc.vector.tensor_tensor(out=res[:], in0=acc.pop((w, half))[:], in1=bias[:, cols], op=ADD)
            nc.sync.dma_start(out=out_rows[w, :, cols], in_=res[:])

        last = UNITS - 1
        widen_attn(0)
        widen_attn(1)
        for u in range(2, LEAD):
            widen_attn(u)
        group_v(0)
        for u in range(TL):
            turn_attn(u)
        for s in range(UNITS):
            if s + LEAD < UNITS:
                widen_attn(s + LEAD)
            if 3 <= s <= 17 and s % 2 == 1:
                empty_w((s - 3) // 2)
            quantize_v(s)
            if s < last:
                group_v(s + 1)
                scale_attn(s)
            else:
                scale_attn(s, 0, 1)
                scale_attn(s, 1, 1)
            if s >= 3 and s % 2 == 1:
                round_o(s - 3, 2)
            g, r = divmod(s - 7, 4)
            if s >= 7 and r == 0:
                empty_o(g)
            if s >= 2 and s % 2 == 0:
                quantize_attn(s // 2 - 1)
            if s == last:
                quantize_attn(s // 2, 0, 2)
            g, r = divmod(s - 9, 4)
            if s >= 9 and r == 0:
                quantize_o(g)
            if s in (11, 12, 19, 20):
                quantize_w((s - 11) // 8, (s - 11) % 2)
            if s + TL < UNITS:
                turn_attn(s + TL)
            if 2 <= s <= 16 and s % 2 == 0:
                turn_w((s - 2) // 2)
            g, r = divmod(s - 6, 4)
            if s >= 6 and r == 0:
                turn_o(g)
            if s >= 2 and s % 2 == 0:
                mix_heads(s - 2)
                mix_heads(s - 1)
            if s in (11, 12):
                spread_bias(s - 11)
            if s in (14, 21):
                project(0, (s - 14) // 7, 0)
                project(0, (s - 14) // 7, 1)
            if s in (16, 22):
                finish(0, (s - 16) // 6)
            if s == 22:
                project(1, 0, 0)
                project(1, 0, 1)
            if s == 23:
                project(1, 1, 0)
                project(1, 1, 1)
        mix_heads(last - 1)
        quantize_attn(last // 2, 2, 1)
        quantize_attn(last // 2, 3, 1)
        quantize_o(4)
        mix_heads(last, 0, 1)
        mix_heads(last, 1, 1)
        round_o(last - 1, 2)
        finish(1, 0)
        turn_o(5)
        project(2, 0, 0)
        empty_o(5)
        finish(1, 1)
        project(2, 1, 0)
        quantize_o(5)
        project(2, 0, 1)
        project(2, 1, 1)
        finish(2, 0)
        finish(2, 1)
